import numpy as np
import ml_dtypes


def mxq(x, axis, fmt="e4m3"):
    dtype, down = {"e4m3": (ml_dtypes.float8_e4m3fn, 7), "e5m2": (ml_dtypes.float8_e5m2, 14)}[fmt]
    v = np.moveaxis(np.asarray(x, np.float32).astype(ml_dtypes.bfloat16).astype(np.float64), axis, -1)
    blocks = v.reshape(v.shape[:-1] + (-1, 32))
    amax = np.abs(blocks).max(-1, keepdims=True)
    byte = np.maximum(np.where(amax > 0, np.frexp(amax)[1] - 1 + 127, 0) - down, 1)
    scale = np.exp2(byte - 127.0)
    codes = (blocks / scale).astype(np.float32).astype(dtype).astype(np.float64)
    return np.moveaxis((codes * scale).reshape(v.shape), -1, axis)


WIDE = False


def mx_kscale(k):
    if not WIDE:
        return np.ones(k)
    levels = np.array([10, -10, 5, -5, 0])
    if k % 512:
        return np.exp2(np.random.permutation(np.resize(levels, k // 32))).repeat(32)
    a = np.empty((k // 512, 16))
    for p in range(k // 512):
        a[p, :8] = np.random.permutation(np.resize(levels, 8))
        for g in range(8):
            far = levels[np.abs(levels - a[p, g]) >= 10]
            a[p, g + 8] = far[np.random.randint(len(far))]
    return np.exp2(a.ravel()).repeat(32)


BF16 = ml_dtypes.bfloat16


def bf(x):
    return np.asarray(x, np.float32).astype(BF16)


def f64(x):
    return np.asarray(x).astype(np.float64)


B, T, HP, WP, NH, G, HD = 2, 2, 8, 16, 16, 4, 32
D = NH * HD
S = HP * WP
AX = HD // 3
E = (NH + 2 * G) * HD
ROPE_THETA = 10000.0
QK_NORM_EPS = 1e-10


def qk_norm(v):
    n = np.sqrt(np.sum(v * v, axis=-1, keepdims=True))
    return v / np.maximum(n, QK_NORM_EPS)


def rope_spatial(v):
    nf, ns, nh, hd = v.shape
    vs = v.reshape(nf, HP, WP, nh, hd).transpose(0, 3, 1, 2, 4)
    inv_freq = 1.0 / (ROPE_THETA ** (np.arange(0, AX, 2, dtype=np.float64) / AX))
    freqs_h = np.arange(HP, dtype=np.float64)[:, None] * inv_freq[None, :]
    freqs_w = np.arange(WP, dtype=np.float64)[:, None] * inv_freq[None, :]
    freqs = freqs_h[:, None, :] + freqs_w[None, :, :]
    cos = np.cos(freqs)[None, None]
    sin = np.sin(freqs)[None, None]
    v_axis = vs[..., :AX]
    v1 = v_axis[..., 0::2]
    v2 = v_axis[..., 1::2]
    rot = np.concatenate([v1 * cos - v2 * sin, v1 * sin + v2 * cos], axis=-1)
    res = np.concatenate([rot, vs[..., AX:]], axis=-1)
    return res.transpose(0, 2, 3, 1, 4).reshape(nf, ns, nh, hd)


def setup_inputs():
    s = mx_kscale(D)
    return {"x": bf(np.random.standard_normal((B, T, S, D)) * s),
            "w_qkv": bf(np.random.standard_normal((E, D)) / np.sqrt(D) / s[None, :])}


def reference(x, w_qkv):
    nf = B * T
    xf = f64(x).reshape(nf, S, D)
    qkv = mxq(xf, 2, "e4m3") @ mxq(f64(w_qkv), 1, "e4m3").T
    q_dim = NH * HD
    g_dim = G * HD
    q = qkv[..., :q_dim].reshape(nf, S, NH, HD)
    k = qkv[..., q_dim:q_dim + g_dim].reshape(nf, S, G, HD)
    v = qkv[..., q_dim + g_dim:].reshape(nf, S, G, HD)
    q_rot = rope_spatial(qk_norm(q))
    k_rot = rope_spatial(qk_norm(k))
    return q_rot, k_rot, v

@@ -1,0 +1,258 @@
+import math
+
+import concourse.mybir as mybir
+from concourse.masks import make_identity
+
+F32 = mybir.dt.float32
+BF16 = mybir.dt.bfloat16
+I32 = mybir.dt.int32
+U32 = mybir.dt.uint32
+U8 = mybir.dt.uint8
+FP8X4 = mybir.dt.float8_e4m3fn_x4
+ALU = mybir.AluOpType
+FUNC = mybir.ActivationFunctionType
+AXIS = mybir.AxisListType
+
+P = 128
+FRAMES = 4
+D = 512
+HALVES = 2
+HD = 32
+HEADS = 16
+GROUPS = 4
+GRID_W = 16
+FREQS = 5
+ROT = 2 * FREQS
+W_TILES = 6
+KEY_TILE = 4
+VALUE_TILE = 5
+BANKS = 8
+UNITS = FRAMES + 1
+POOL_UNITS = 3
+VECTOR_COPIES = 3
+ROPE_THETA = 10000.0
+QK_NORM_EPS = 1e-10
+ROUND_MAGIC = 12582912.0
+
+FLOPS = 2 * FRAMES * P * D * W_TILES * P
+
+
+def tile_spatiotemporalattention_pa_s_kernel(tc, x, w_qkv, out_0, out_1, out_2):
+    nc = tc.nc
+    x_tiles = x.rearrange("b t s d -> s (b t) d")
+    w_tiles = w_qkv.rearrange("(t r) d -> r t d", r=P)
+
+    with tc.tile_pool(name="keep", bufs=1) as keep, tc.tile_pool(
+        name="unit", bufs=UNITS
+    ) as unit, tc.psum_pool(name="psum", bufs=BANKS) as psum, tc.manual_schedule():
+        x_sb = keep.tile([P, FRAMES, D], BF16)
+        w_sb = keep.tile([P, W_TILES, D], BF16)
+        nc.sync.dma_start(out=x_sb[:, 0, :], in_=x_tiles[:, 0, :])
+        for t in range(KEY_TILE):
+            nc.sync.dma_start(out=w_sb[:, t, :], in_=w_tiles[:, t, :])
+        for f in range(1, FRAMES):
+            nc.sync.dma_start(out=x_sb[:, f, :], in_=x_tiles[:, f, :])
+        for t in (KEY_TILE, VALUE_TILE):
+            nc.sync.dma_start(out=w_sb[:, t, :], in_=w_tiles[:, t, :])
+
+        zero = keep.tile([P, 1], F32)
+        nc.vector.memset(zero[:], 0.0)
+        warm_sin = keep.tile([P, 1], F32)
+        nc.scalar.activation(out=warm_sin[:], in_=zero[:], func=FUNC.Sin)
+
+        patch = keep.tile([P, 1], I32)
+        nc.gpsimd.iota(patch[:], pattern=[[0, 1]], base=0, channel_multiplier=1)
+        ident = keep.tile([P, P], F32)
+        make_identity(nc, ident[:])
+
+        grid_row = keep.tile([P, 1], I32)
+        nc.vector.tensor_single_scalar(
+            out=grid_row[:], in_=patch[:], scalar=4, op=ALU.arith_shift_right
+        )
+        steps = keep.tile([P, 1], F32)
+        nc.vector.scalar_tensor_tensor(
+            out=steps[:],
+            in0=grid_row[:],
+            scalar=float(1 - GRID_W),
+            in1=patch[:],
+            op0=ALU.mult,
+            op1=ALU.add,
+        )
+        quarter = keep.tile([P, 2], F32)
+        nc.vector.memset(quarter[:, 0:1], 0.25)
+        nc.vector.memset(quarter[:, 1:2], 0.0)
+        turns = keep.tile([P, 2, FREQS], F32)
+        for m in range(FREQS):
+            nc.vector.scalar_tensor_tensor(
+                out=turns[:, :, m],
+                in0=steps[:, 0:1].to_broadcast([P, 2]),
+                scalar=ROPE_THETA ** (-2.0 * m / ROT) / (2.0 * math.pi),
+                in1=quarter[:],
+                op0=ALU.mult,
+                op1=ALU.add,
+            )
+        whole = keep.tile([P, 2, FREQS], F32)
+        nc.vector.tensor_scalar(
+            out=whole[:],
+            in0=turns[:],
+            scalar1=ROUND_MAGIC,
+            scalar2=ROUND_MAGIC,
+            op0=ALU.add,
+            op1=ALU.subtract,
+        )
+        part = keep.tile([P, 2, FREQS], F32)
+        nc.vector.tensor_tensor(out=part[:], in0=turns[:], in1=whole[:], op=ALU.subtract)
+        table = keep.tile([P, 3, FREQS], F32)
+        nc.scalar.activation(out=table[:, 1:3, :], in_=part[:], func=FUNC.Sin, scale=2.0 * math.pi)
+        nc.scalar.activation(
+            out=table[:, 0, :], in_=part[:, 1, :], func=FUNC.Sin, scale=-2.0 * math.pi
+        )
+        cos_sin = table[:, 1:3, :].unsqueeze(1).to_broadcast([P, HEADS, 2, FREQS])
+        nsin_cos = table[:, 0:2, :].unsqueeze(1).to_broadcast([P, HEADS, 2, FREQS])
+        one = keep.tile([P, 1], F32)
+        nc.vector.memset(one[:], 1.0)
+        warm_rsqrt = keep.tile([P, 1], F32)
+        nc.scalar.activation(out=warm_rsqrt[:], in_=one[:], func=FUNC.Abs_reciprocal_sqrt)
+
+        x_op = (
+            x_sb,
+            keep.tile([P, FRAMES * D], BF16, align_bytes=64, name="x_grouped"),
+            keep.tile([P, FRAMES * P], U32, align_bytes=64, name="x_codes"),
+            keep.tile([P, FRAMES * P], U8, align_bytes=64, name="x_scales"),
+        )
+        w_op = (
+            w_sb,
+            keep.tile([P, W_TILES * D], BF16, align_bytes=64, name="w_grouped"),
+            keep.tile([P, W_TILES * P], U32, align_bytes=64, name="w_codes"),
+            keep.tile([P, W_TILES * P], U8, align_bytes=64, name="w_scales"),
+        )
+
+        def quantise_tile(operand, t, copy):
+            rows, grouped, codes, scales = operand
+            words = rows[:, t, :].bitcast(F32)
+            flipped = psum.tile([P, HALVES, P], F32, tag="bank")
+            for u in range(HALVES):
+                nc.tensor.transpose(flipped[:, u, :], words[:, u::HALVES], ident[:])
+            copy(
+                out=grouped[:, t * D : (t + 1) * D]
+                .bitcast(F32)
+                .rearrange("p (r u) -> p r u", u=HALVES),
+                in_=flipped[:].rearrange("p u r -> p r u"),
+            )
+            nc.vector.quantize_mx(
+                out=codes[:, t * P : (t + 1) * P].bitcast(FP8X4),
+                scales=scales[:, t * P : (t + 1) * P],
+                in_=grouped[:, t * D : (t + 1) * D],
+            )
+
+        in_load_order = (
+            [(x_op, 0)]
+            + [(w_op, t) for t in range(KEY_TILE)]
+            + [(x_op, f) for f in range(1, FRAMES)]
+            + [(w_op, KEY_TILE), (w_op, VALUE_TILE)]
+        )
+        for n, (operand, t) in enumerate(in_load_order):
+            quantise_tile(
+                operand, t, nc.vector.tensor_copy if n < VECTOR_COPIES else nc.scalar.copy
+            )
+
+        def project(out, frame, first_tile, tiles):
+            cols = slice(first_tile * P, (first_tile + tiles) * P)
+            nc.tensor.matmul_mx(
+                out=out,
+                lhsT=x_op[2][:, frame * P : (frame + 1) * P].bitcast(FP8X4),
+                lhsT_scale=x_op[3][:, frame * P : (frame + 1) * P],
+                rhs=w_op[2][:, cols].bitcast(FP8X4),
+                rhs_scale=w_op[3][:, cols],
+                start=True,
+                stop=True,
+            )
+
+        q_raws = []
+        for f in range(FRAMES):
+            q_raw = psum.tile([P, HEADS, HD], F32, tag="bank")
+            project(q_raw[:].rearrange("p h c -> p (h c)"), f, 0, KEY_TILE)
+            q_raws.append(q_raw)
+        k_raw = psum.tile([P, FRAMES, GROUPS * HD], F32, tag="bank")
+        v_raw = psum.tile([P, FRAMES, GROUPS * HD], F32, tag="bank")
+        for f in range(FRAMES):
+            project(k_raw[:, f, :], f, KEY_TILE, 1)
+        for f in range(FRAMES):
+            project(v_raw[:, f, :], f, VALUE_TILE, 1)
+        raws = q_raws + [k_raw[:].rearrange("p f (g c) -> p (f g) c", c=HD)]
+
+        sumsqs = []
+        results = []
+
+        def square_and_sum(u):
+            squares = unit.tile([P, HEADS, HD], F32)
+            nc.scalar.activation(out=squares[:], in_=raws[u][:], func=FUNC.Square)
+            sumsq = unit.tile([P, HEADS], F32)
+            nc.vector.tensor_reduce(out=sumsq[:], in_=squares[:], axis=AXIS.X, op=ALU.add)
+            sumsqs.append(sumsq)
+
+        def normalise(u):
+            inv = unit.tile([P, HEADS], F32)
+            nc.scalar.activation(out=inv[:], in_=sumsqs[u][:], func=FUNC.Abs_reciprocal_sqrt)
+            res = unit.tile([P, HEADS, HD], F32)
+            nc.vector.scalar_tensor_tensor(
+                out=res[:],
+                in0=inv[:].unsqueeze(2).to_broadcast([P, HEADS, HD]),
+                scalar=1.0 / QK_NORM_EPS,
+                in1=raws[u][:],
+                op0=ALU.min,
+                op1=ALU.mult,
+            )
+            results.append(res)
+
+        def rotate_and_store(units, engine, queue):
+            from_even = {}
+            from_odd = {}
+            for u in units:
+                pairs = results[u][:, :, 0:ROT].rearrange("p h (m e) -> p h m e", e=2)
+                from_even[u] = unit.tile([P, HEADS, 2, FREQS], F32, name="from_even")
+                engine.tensor_tensor(
+                    out=from_even[u][:],
+                    in0=pairs[:, :, :, 0].unsqueeze(2).to_broadcast([P, HEADS, 2, FREQS]),
+                    in1=cos_sin,
+                    op=ALU.mult,
+                )
+            for u in units:
+                pairs = results[u][:, :, 0:ROT].rearrange("p h (m e) -> p h m e", e=2)
+                from_odd[u] = unit.tile([P, HEADS, 2, FREQS], F32, name="from_odd")
+                engine.tensor_tensor(
+                    out=from_odd[u][:],
+                    in0=pairs[:, :, :, 1].unsqueeze(2).to_broadcast([P, HEADS, 2, FREQS]),
+                    in1=nsin_cos,
+                    op=ALU.mult,
+                )
+            for u in units:
+                engine.tensor_tensor(
+                    out=results[u][:, :, 0:ROT].rearrange("p h (o m) -> p h o m", o=2),
+                    in0=from_even[u][:],
+                    in1=from_odd[u][:],
+                    op=ALU.add,
+                )
+                if u < FRAMES:
+                    queue.dma_start(out=out_0[u], in_=results[u][:])
+                else:
+                    queue.dma_start(
+                        out=out_1.rearrange("f s g c -> s f (g c)"),
+                        in_=results[u][:].rearrange("p (f g) c -> p f (g c)", f=FRAMES),
+                    )
+
+        def copy_values():
+            v_res = keep.tile([P, FRAMES, GROUPS * HD], F32)
+            nc.scalar.copy(out=v_res[:], in_=v_raw[:])
+            nc.scalar.dma_start(out=out_2.rearrange("f s g c -> s f (g c)"), in_=v_res[:])
+
+        square_and_sum(0)
+        for u in range(UNITS):
+            if u + 1 < UNITS:
+                square_and_sum(u + 1)
+            if u + 1 == UNITS - 1:
+                copy_values()
+            normalise(u)
+            if u < POOL_UNITS:
+                rotate_and_store([u], nc.gpsimd, nc.sync)
+        rotate_and_store(list(range(POOL_UNITS, UNITS)), nc.vector, nc.scalar)

@@ -78,20 +78,21 @@ def tile_spatiotemporalattention_pa_s_kernel(tc, x, w_qkv, out_0, out_1, out_2):
             op0=ALU.mult,
             op1=ALU.add,
         )
-        quarter = keep.tile([P, 2], F32)
-        nc.vector.memset(quarter[:, 0:1], 0.25)
-        nc.vector.memset(quarter[:, 1:2], 0.0)
-        turns = keep.tile([P, 2, FREQS], F32)
+        quarters = keep.tile([P, 2, 2], F32)
+        nc.vector.memset(quarters[:], 0.25)
+        nc.vector.memset(quarters[:, 0, 1:2], 0.5)
+        nc.vector.memset(quarters[:, 1, 0:1], 0.0)
+        turns = keep.tile([P, 2, FREQS, 2], F32)
         for m in range(FREQS):
             nc.vector.scalar_tensor_tensor(
-                out=turns[:, :, m],
-                in0=steps[:, 0:1].to_broadcast([P, 2]),
+                out=turns[:, :, m, :],
+                in0=steps[:, 0:1].unsqueeze(2).to_broadcast([P, 2, 2]),
                 scalar=ROPE_THETA ** (-2.0 * m / ROT) / (2.0 * math.pi),
-                in1=quarter[:],
+                in1=quarters[:],
                 op0=ALU.mult,
                 op1=ALU.add,
             )
-        whole = keep.tile([P, 2, FREQS], F32)
+        whole = keep.tile([P, 2, FREQS, 2], F32)
         nc.vector.tensor_scalar(
             out=whole[:],
             in0=turns[:],
@@ -100,15 +101,16 @@ def tile_spatiotemporalattention_pa_s_kernel(tc, x, w_qkv, out_0, out_1, out_2):
             op0=ALU.add,
             op1=ALU.subtract,
         )
-        part = keep.tile([P, 2, FREQS], F32)
+        part = keep.tile([P, 2, FREQS, 2], F32)
         nc.vector.tensor_tensor(out=part[:], in0=turns[:], in1=whole[:], op=ALU.subtract)
-        table = keep.tile([P, 3, FREQS], F32)
-        nc.scalar.activation(out=table[:, 1:3, :], in_=part[:], func=FUNC.Sin, scale=2.0 * math.pi)
+        table = keep.tile([P, 2, ROT], F32)
         nc.scalar.activation(
-            out=table[:, 0, :], in_=part[:, 1, :], func=FUNC.Sin, scale=-2.0 * math.pi
+            out=table[:],
+            in_=part[:].rearrange("p o m e -> p o (m e)"),
+            func=FUNC.Sin,
+            scale=2.0 * math.pi,
         )
-        cos_sin = table[:, 1:3, :].unsqueeze(1).to_broadcast([P, HEADS, 2, FREQS])
-        nsin_cos = table[:, 0:2, :].unsqueeze(1).to_broadcast([P, HEADS, 2, FREQS])
+        factors = table[:].unsqueeze(1).to_broadcast([P, HEADS, 2, ROT])
         one = keep.tile([P, 1], F32)
         nc.vector.memset(one[:], 1.0)
         warm_rsqrt = keep.tile([P, 1], F32)
@@ -206,31 +208,21 @@ def tile_spatiotemporalattention_pa_s_kernel(tc, x, w_qkv, out_0, out_1, out_2):
             results.append(res)
 
         def rotate_and_store(units, engine, queue):
-            from_even = {}
-            from_odd = {}
+            products = {}
             for u in units:
-                pairs = results[u][:, :, 0:ROT].rearrange("p h (m e) -> p h m e", e=2)
-                from_even[u] = unit.tile([P, HEADS, 2, FREQS], F32, name="from_even")
+                products[u] = unit.tile([P, HEADS, 2, ROT], F32, name="products")
                 engine.tensor_tensor(
-                    out=from_even[u][:],
-                    in0=pairs[:, :, :, 0].unsqueeze(2).to_broadcast([P, HEADS, 2, FREQS]),
-                    in1=cos_sin,
+                    out=products[u][:],
+                    in0=results[u][:, :, 0:ROT].unsqueeze(2).to_broadcast([P, HEADS, 2, ROT]),
+                    in1=factors,
                     op=ALU.mult,
                 )
             for u in units:
-                pairs = results[u][:, :, 0:ROT].rearrange("p h (m e) -> p h m e", e=2)
-                from_odd[u] = unit.tile([P, HEADS, 2, FREQS], F32, name="from_odd")
+                pairs = products[u][:].rearrange("p h o (m e) -> p h (o m) e", e=2)
                 engine.tensor_tensor(
-                    out=from_odd[u][:],
-                    in0=pairs[:, :, :, 1].unsqueeze(2).to_broadcast([P, HEADS, 2, FREQS]),
-                    in1=nsin_cos,
-                    op=ALU.mult,
-                )
-            for u in units:
-                engine.tensor_tensor(
-                    out=results[u][:, :, 0:ROT].rearrange("p h (o m) -> p h o m", o=2),
-                    in0=from_even[u][:],
-                    in1=from_odd[u][:],
+                    out=results[u][:, :, 0:ROT],
+                    in0=pairs[:, :, :, 0],
+                    in1=pairs[:, :, :, 1],
                     op=ALU.add,
                 )
                 if u < FRAMES:

import math

import concourse.mybir as mybir
from concourse.masks import make_identity

F32 = mybir.dt.float32
BF16 = mybir.dt.bfloat16
I32 = mybir.dt.int32
U32 = mybir.dt.uint32
U8 = mybir.dt.uint8
FP8X4 = mybir.dt.float8_e4m3fn_x4
ALU = mybir.AluOpType
FUNC = mybir.ActivationFunctionType
AXIS = mybir.AxisListType

P = 128
FRAMES = 4
D = 512
HALVES = 2
HD = 32
HEADS = 16
GROUPS = 4
GRID_W = 16
FREQS = 5
ROT = 2 * FREQS
W_TILES = 6
KEY_TILE = 4
VALUE_TILE = 5
BANKS = 8
UNITS = FRAMES + 1
POOL_UNITS = 3
VECTOR_COPIES = 3
ROPE_THETA = 10000.0
QK_NORM_EPS = 1e-10
ROUND_MAGIC = 12582912.0

FLOPS = 2 * FRAMES * P * D * W_TILES * P


def tile_spatiotemporalattention_pa_s_kernel(tc, x, w_qkv, out_0, out_1, out_2):
    nc = tc.nc
    x_tiles = x.rearrange("b t s d -> s (b t) d")
    w_tiles = w_qkv.rearrange("(t r) d -> r t d", r=P)

    with tc.tile_pool(name="keep", bufs=1) as keep, tc.tile_pool(
        name="unit", bufs=UNITS
    ) as unit, tc.psum_pool(name="psum", bufs=BANKS) as psum, tc.manual_schedule():
        x_sb = keep.tile([P, FRAMES, D], BF16)
        w_sb = keep.tile([P, W_TILES, D], BF16)
        nc.sync.dma_start(out=x_sb[:, 0, :], in_=x_tiles[:, 0, :])
        for t in range(KEY_TILE):
            nc.sync.dma_start(out=w_sb[:, t, :], in_=w_tiles[:, t, :])
        for f in range(1, FRAMES):
            nc.sync.dma_start(out=x_sb[:, f, :], in_=x_tiles[:, f, :])
        for t in (KEY_TILE, VALUE_TILE):
            nc.sync.dma_start(out=w_sb[:, t, :], in_=w_tiles[:, t, :])

        zero = keep.tile([P, 1], F32)
        nc.vector.memset(zero[:], 0.0)
        warm_sin = keep.tile([P, 1], F32)
        nc.scalar.activation(out=warm_sin[:], in_=zero[:], func=FUNC.Sin)

        patch = keep.tile([P, 1], I32)
        nc.gpsimd.iota(patch[:], pattern=[[0, 1]], base=0, channel_multiplier=1)
        ident = keep.tile([P, P], F32)
        make_identity(nc, ident[:])

        grid_row = keep.tile([P, 1], I32)
        nc.vector.tensor_single_scalar(
            out=grid_row[:], in_=patch[:], scalar=4, op=ALU.arith_shift_right
        )
        steps = keep.tile([P, 1], F32)
        nc.vector.scalar_tensor_tensor(
            out=steps[:],
            in0=grid_row[:],
            scalar=float(1 - GRID_W),
            in1=patch[:],
            op0=ALU.mult,
            op1=ALU.add,
        )
        quarters = keep.tile([P, 2, 2], F32)
        nc.vector.memset(quarters[:], 0.25)
        nc.vector.memset(quarters[:, 0, 1:2], 0.5)
        nc.vector.memset(quarters[:, 1, 0:1], 0.0)
        turns = keep.tile([P, 2, FREQS, 2], F32)
        for m in range(FREQS):
            nc.vector.scalar_tensor_tensor(
                out=turns[:, :, m, :],
                in0=steps[:, 0:1].unsqueeze(2).to_broadcast([P, 2, 2]),
                scalar=ROPE_THETA ** (-2.0 * m / ROT) / (2.0 * math.pi),
                in1=quarters[:],
                op0=ALU.mult,
                op1=ALU.add,
            )
        whole = keep.tile([P, 2, FREQS, 2], F32)
        nc.vector.tensor_scalar(
            out=whole[:],
            in0=turns[:],
            scalar1=ROUND_MAGIC,
            scalar2=ROUND_MAGIC,
            op0=ALU.add,
            op1=ALU.subtract,
        )
        part = keep.tile([P, 2, FREQS, 2], F32)
        nc.vector.tensor_tensor(out=part[:], in0=turns[:], in1=whole[:], op=ALU.subtract)
        table = keep.tile([P, 2, ROT], F32)
        nc.scalar.activation(
            out=table[:],
            in_=part[:].rearrange("p o m e -> p o (m e)"),
            func=FUNC.Sin,
            scale=2.0 * math.pi,
        )
        factors = table[:].unsqueeze(1).to_broadcast([P, HEADS, 2, ROT])
        one = keep.tile([P, 1], F32)
        nc.vector.memset(one[:], 1.0)
        warm_rsqrt = keep.tile([P, 1], F32)
        nc.scalar.activation(out=warm_rsqrt[:], in_=one[:], func=FUNC.Abs_reciprocal_sqrt)

        x_op = (
            x_sb,
            keep.tile([P, FRAMES * D], BF16, align_bytes=64, name="x_grouped"),
            keep.tile([P, FRAMES * P], U32, align_bytes=64, name="x_codes"),
            keep.tile([P, FRAMES * P], U8, align_bytes=64, name="x_scales"),
        )
        w_op = (
            w_sb,
            keep.tile([P, W_TILES * D], BF16, align_bytes=64, name="w_grouped"),
            keep.tile([P, W_TILES * P], U32, align_bytes=64, name="w_codes"),
            keep.tile([P, W_TILES * P], U8, align_bytes=64, name="w_scales"),
        )

        def quantise_tile(operand, t, copy):
            rows, grouped, codes, scales = operand
            words = rows[:, t, :].bitcast(F32)
            flipped = psum.tile([P, HALVES, P], F32, tag="bank")
            for u in range(HALVES):
                nc.tensor.transpose(flipped[:, u, :], words[:, u::HALVES], ident[:])
            copy(
                out=grouped[:, t * D : (t + 1) * D]
                .bitcast(F32)
                .rearrange("p (r u) -> p r u", u=HALVES),
                in_=flipped[:].rearrange("p u r -> p r u"),
            )
            nc.vector.quantize_mx(
                out=codes[:, t * P : (t + 1) * P].bitcast(FP8X4),
                scales=scales[:, t * P : (t + 1) * P],
                in_=grouped[:, t * D : (t + 1) * D],
            )

        in_load_order = (
            [(x_op, 0)]
            + [(w_op, t) for t in range(KEY_TILE)]
            + [(x_op, f) for f in range(1, FRAMES)]
            + [(w_op, KEY_TILE), (w_op, VALUE_TILE)]
        )
        for n, (operand, t) in enumerate(in_load_order):
            quantise_tile(
                operand, t, nc.vector.tensor_copy if n < VECTOR_COPIES else nc.scalar.copy
            )

        def project(out, frame, first_tile, tiles):
            cols = slice(first_tile * P, (first_tile + tiles) * P)
            nc.tensor.matmul_mx(
                out=out,
                lhsT=x_op[2][:, frame * P : (frame + 1) * P].bitcast(FP8X4),
                lhsT_scale=x_op[3][:, frame * P : (frame + 1) * P],
                rhs=w_op[2][:, cols].bitcast(FP8X4),
                rhs_scale=w_op[3][:, cols],
                start=True,
                stop=True,
            )

        q_raws = []
        for f in range(FRAMES):
            q_raw = psum.tile([P, HEADS, HD], F32, tag="bank")
            project(q_raw[:].rearrange("p h c -> p (h c)"), f, 0, KEY_TILE)
            q_raws.append(q_raw)
        k_raw = psum.tile([P, FRAMES, GROUPS * HD], F32, tag="bank")
        v_raw = psum.tile([P, FRAMES, GROUPS * HD], F32, tag="bank")
        for f in range(FRAMES):
            project(k_raw[:, f, :], f, KEY_TILE, 1)
        for f in range(FRAMES):
            project(v_raw[:, f, :], f, VALUE_TILE, 1)
        raws = q_raws + [k_raw[:].rearrange("p f (g c) -> p (f g) c", c=HD)]

        sumsqs = []
        results = []

        def square_and_sum(u):
            squares = unit.tile([P, HEADS, HD], F32)
            nc.scalar.activation(out=squares[:], in_=raws[u][:], func=FUNC.Square)
            sumsq = unit.tile([P, HEADS], F32)
            nc.vector.tensor_reduce(out=sumsq[:], in_=squares[:], axis=AXIS.X, op=ALU.add)
            sumsqs.append(sumsq)

        def normalise(u):
            inv = unit.tile([P, HEADS], F32)
            nc.scalar.activation(out=inv[:], in_=sumsqs[u][:], func=FUNC.Abs_reciprocal_sqrt)
            res = unit.tile([P, HEADS, HD], F32)
            nc.vector.scalar_tensor_tensor(
                out=res[:],
                in0=inv[:].unsqueeze(2).to_broadcast([P, HEADS, HD]),
                scalar=1.0 / QK_NORM_EPS,
                in1=raws[u][:],
                op0=ALU.min,
                op1=ALU.mult,
            )
            results.append(res)

        def rotate_and_store(units, engine, queue):
            products = {}
            for u in units:
                products[u] = unit.tile([P, HEADS, 2, ROT], F32, name="products")
                engine.tensor_tensor(
                    out=products[u][:],
                    in0=results[u][:, :, 0:ROT].unsqueeze(2).to_broadcast([P, HEADS, 2, ROT]),
                    in1=factors,
                    op=ALU.mult,
                )
            for u in units:
                pairs = products[u][:].rearrange("p h o (m e) -> p h (o m) e", e=2)
                engine.tensor_tensor(
                    out=results[u][:, :, 0:ROT],
                    in0=pairs[:, :, :, 0],
                    in1=pairs[:, :, :, 1],
                    op=ALU.add,
                )
                if u < FRAMES:
                    queue.dma_start(out=out_0[u], in_=results[u][:])
                else:
                    queue.dma_start(
                        out=out_1.rearrange("f s g c -> s f (g c)"),
                        in_=results[u][:].rearrange("p (f g) c -> p f (g c)", f=FRAMES),
                    )

        def copy_values():
            v_res = keep.tile([P, FRAMES, GROUPS * HD], F32)
            nc.scalar.copy(out=v_res[:], in_=v_raw[:])
            nc.scalar.dma_start(out=out_2.rearrange("f s g c -> s f (g c)"), in_=v_res[:])

        square_and_sum(0)
        for u in range(UNITS):
            if u + 1 < UNITS:
                square_and_sum(u + 1)
            if u + 1 == UNITS - 1:
                copy_values()
            normalise(u)
            if u < POOL_UNITS:
                rotate_and_store([u], nc.gpsimd, nc.sync)
        rotate_and_store(list(range(POOL_UNITS, UNITS)), nc.vector, nc.scalar)
